import numpy as np
import ml_dtypes


def mxq(x, axis, fmt="e4m3"):
    dtype, down = {"e4m3": (ml_dtypes.float8_e4m3fn, 7), "e5m2": (ml_dtypes.float8_e5m2, 14)}[fmt]
    v = np.moveaxis(np.asarray(x, np.float32).astype(ml_dtypes.bfloat16).astype(np.float64), axis, -1)
    blocks = v.reshape(v.shape[:-1] + (-1, 32))
    amax = np.abs(blocks).max(-1, keepdims=True)
    byte = np.maximum(np.where(amax > 0, np.frexp(amax)[1] - 1 + 127, 0) - down, 1)
    scale = np.exp2(byte - 127.0)
    codes = (blocks / scale).astype(np.float32).astype(dtype).astype(np.float64)
    return np.moveaxis((codes * scale).reshape(v.shape), -1, axis)


WIDE = False


def mx_kscale(k):
    if not WIDE:
        return np.ones(k)
    levels = np.array([10, -10, 5, -5, 0])
    if k % 512:
        return np.exp2(np.random.permutation(np.resize(levels, k // 32))).repeat(32)
    a = np.empty((k // 512, 16))
    for p in range(k // 512):
        a[p, :8] = np.random.permutation(np.resize(levels, 8))
        for g in range(8):
            far = levels[np.abs(levels - a[p, g]) >= 10]
            a[p, g + 8] = far[np.random.randint(len(far))]
    return np.exp2(a.ravel()).repeat(32)


BF16 = ml_dtypes.bfloat16


def bf(x):
    return np.asarray(x, np.float32).astype(BF16)


def f64(x):
    return np.asarray(x).astype(np.float64)


E2M1 = np.array([0.0, 0.5, 1.0, 1.5, 2.0, 3.0, 4.0, 6.0, -0.0, -0.5, -1.0, -1.5, -2.0, -3.0, -4.0, -6.0])


def pack_weight(w, fmt):
    k, n = w.shape
    w = f64(bf(w)).reshape(k // 32, 32, n)
    amax = np.abs(w).max(1)
    if fmt == "e4m3":
        byte = np.frexp(amax)[1] - 1 + 127 - 7
    else:
        mant, ex = np.frexp(amax / 6.0)
        byte = np.where(mant > 0.5, ex, ex - 1) + 127
    byte = np.clip(np.where(amax > 0, byte, 1), 1, 254)
    scaled = (w * np.exp2(127.0 - byte)[:, None, :]).reshape(k, n).astype(np.float32)
    by_word = np.ascontiguousarray(scaled.reshape(k // 512, 128, 4, n).transpose(0, 1, 3, 2))
    if fmt == "e4m3":
        words = by_word.astype(ml_dtypes.float8_e4m3fn).view(np.uint8)
    else:
        c = by_word.astype(ml_dtypes.float4_e2m1fn).view(np.uint8) & 0xF
        words = c[..., 0::2] | (c[..., 1::2] << 4)
    return np.ascontiguousarray(words), np.ascontiguousarray(byte.astype(np.uint8).reshape(k // 512, 16, n))


def unpack_weight(words, scales, fmt):
    g, p, n, _ = words.shape
    if fmt == "e4m3":
        vals = np.ascontiguousarray(words).view(ml_dtypes.float8_e4m3fn).astype(np.float64)
    else:
        nib = np.empty((g, p, n, 4), np.uint8)
        nib[..., 0::2] = words & 0xF
        nib[..., 1::2] = words >> 4
        vals = E2M1[nib]
    vals = vals * np.repeat(np.exp2(scales.astype(np.float64) - 127.0), 8, axis=1)[..., None]
    return vals.transpose(0, 1, 3, 2).reshape(g * 512, n)
def pack4(w):
    words, scales = pack_weight(w, "e2m1")
    return words.reshape(words.shape[0], 128, -1), scales


def unpack4(words, scales):
    return unpack_weight(words.reshape(words.shape[0], 128, -1, 2), scales, "e2m1")


N, C0, H, KS, P, C, O, F, NC = 512, 1, 4, 3, 2, 512, 512, 512, 10
KK = KS * KS
OH = H - KS + 1
OP = OH // P
FC = O * OP * OP


def relu(v):
    return np.maximum(v, 0.0)


def maxpool(v):
    n, c, hh, ww = v.shape
    hp, wp = hh // P, ww // P
    return v[:, :, :hp * P, :wp * P].reshape(n, c, hp, P, wp, P).max(axis=(3, 5))


def draw0():
    s = mx_kscale(C)
    t = mx_kscale(FC)
    tt = np.repeat(np.repeat(t.reshape(O, OP, OP), P, axis=1), P, axis=2)
    h = np.maximum(np.random.standard_normal((P * P, N, C, H, H)).max(0), 0.0)
    h_pool1 = bf(h * s[None, :, None, None])
    w2 = bf(np.random.standard_normal((O, C, KK, OH, OH)) * 0.8 / np.sqrt(KK * C) / s[None, :, None, None, None] * tt[:, None, None, :, :])
    b2 = bf(np.random.standard_normal((O, OH, OH)) * 0.3 * tt)
    fc1_w_words, fc1_w_scales = pack4(np.random.standard_normal((FC, F)) * 0.8 / np.sqrt(FC) / t[:, None])
    return {
        "h_pool1": h_pool1,
        "w2": w2,
        "b2": b2,
        "fc1_w_words": fc1_w_words,
        "fc1_w_scales": fc1_w_scales,
        "fc1_b": bf(np.random.standard_normal(F) * 0.3),
    }


def core(h_pool1, w2, b2, fc1_w_words, fc1_w_scales, fc1_b):
    hq = mxq(f64(h_pool1).transpose(2, 3, 0, 1), 3, "e4m3")
    wq = mxq(f64(w2).transpose(2, 3, 4, 1, 0), 3, "e4m3")
    y = sum((hq[i:i + OH, j:j + OH] @ wq[i * KS + j]) for i in range(KS) for j in range(KS))
    y = y.transpose(2, 3, 0, 1) + f64(b2)
    g = maxpool(relu(y)).reshape(N, FC)
    return relu((mxq(g, 1, "e4m3") @ unpack4(fc1_w_words, fc1_w_scales)) + f64(fc1_b))


def e4m3fn_bytes(y):
    return np.clip(np.asarray(y, np.float64), -448.0, 448.0).astype(np.float32).astype(ml_dtypes.float8_e4m3fn).view(np.uint8)


def e4m3fn_values(b):
    return np.asarray(b, np.uint8).view(ml_dtypes.float8_e4m3fn).astype(np.float64)


def setup_inputs():
    d = draw0()
    x0 = np.asarray(d['h_pool1']).astype(np.float64)
    s = (np.max(np.abs(x0), axis=(0, 2, 3), keepdims=True) / 448.0).astype(np.float32)
    out = {}
    for k, v in d.items():
        if k == 'h_pool1':
            out['h_pool1_bytes'] = e4m3fn_bytes(x0 / s.astype(np.float64))
            out['h_pool1_scale'] = s
        else:
            out[k] = v
    return out


def reference(h_pool1_bytes, h_pool1_scale, w2, b2, fc1_w_words, fc1_w_scales, fc1_b):
    return core(e4m3fn_values(h_pool1_bytes) * h_pool1_scale.astype(np.float64), w2, b2, fc1_w_words, fc1_w_scales, fc1_b)

@@ -1,0 +1,292 @@
+from contextlib import ExitStack
+
+import concourse.mybir as mybir
+from concourse.masks import make_identity
+
+N, C, PX, O, F = 512, 512, 16, 512, 512
+FLOPS = 2 * N * C * 9 * 4 * O + 2 * N * O * F
+
+F32 = mybir.dt.float32
+BF16 = mybir.dt.bfloat16
+U32 = mybir.dt.uint32
+I32 = mybir.dt.int32
+U8 = mybir.dt.uint8
+FP8 = mybir.dt.float8_e4m3fn
+E4X4 = mybir.dt.float8_e4m3fn_x4
+E2X4 = mybir.dt.float4_e2m1fn_x4
+ALU = mybir.AluOpType
+ACT = mybir.ActivationFunctionType
+
+P = 128
+OFFS = 9
+BIG, HU, HB, WB, WC, TR, AC = 2, 4, 3, 4, 12, 3, 5
+
+
+def tile_locallyconnectednet_pa_t_w4_kernel(
+    tc, h_bytes, h_scale, w2, b2, fc1_words, fc1_scales, fc1_b, out
+):
+    nc = tc.nc
+    h_rows = h_bytes.rearrange("(b n) c x y -> b n (c x y)", n=P)
+    w_rows = w2.rearrange("(m u) (p t) k i j -> u p m (t k i j)", u=4, t=4)
+
+    with ExitStack() as ctx:
+        const = ctx.enter_context(tc.tile_pool(name="const", bufs=1))
+        big = ctx.enter_context(tc.tile_pool(name="big", bufs=BIG))
+        hup = ctx.enter_context(tc.tile_pool(name="hup", bufs=HU))
+        hnp = ctx.enter_context(tc.tile_pool(name="hnp", bufs=2))
+        hbp = ctx.enter_context(tc.tile_pool(name="hbp", bufs=HB))
+        wbp = ctx.enter_context(tc.tile_pool(name="wbp", bufs=WB))
+        codes_pool = ctx.enter_context(tc.tile_pool(name="codes", bufs=WC))
+        tail = ctx.enter_context(tc.tile_pool(name="tail", bufs=2))
+        trp = ctx.enter_context(tc.psum_pool(name="trp", bufs=TR))
+        accp = ctx.enter_context(tc.psum_pool(name="accp", bufs=AC))
+
+        ident = const.tile([P, P], F32, name="ident")
+        make_identity(nc, ident[:])
+        sc = const.tile([P, 4], F32, name="sc")
+        hcodes = const.tile([P, PX, N], U32, name="hcodes", align_bytes=64)
+        hscales = const.tile([P, PX, N], U8, name="hscales", align_bytes=64)
+        gbf = const.tile([P, 4, N], BF16, name="gbf", align_bytes=64)
+        b2b = const.tile([P, 16], BF16, name="b2b")
+        b2f = const.tile([P, 16], F32, name="b2f")
+        fw = const.tile([P, 1024], U8, name="fw", align_bytes=64)
+        fs = const.tile([P, F], U8, name="fs", align_bytes=64)
+        fb = const.tile([P, F], BF16, name="fb")
+        nc.gpsimd.memset(fs[:].bitcast(I32), 0)
+
+        hu = {}
+        hn_tiles = {}
+        hb_tiles = {}
+
+        def load_h(b):
+            for half in range(2):
+                hu_tile = hup.tile([P, 4096], U8, name="hu", align_bytes=64)
+                nc.sync.dma_start(out=hu_tile[:], in_=h_rows[b][:, half * 4096 : (half + 1) * 4096])
+                hu[b, half] = hu_tile
+
+        def cast_h(b, half, engine):
+            if b not in hn_tiles:
+                hn = hnp.tile([P, 8192], BF16, name="hn", align_bytes=64)
+                hn_tiles[b] = hn
+            src = hu[b, half][:].bitcast(FP8)
+            dst = hn_tiles[b][:, half * 4096 : (half + 1) * 4096]
+            if engine == "S":
+                nc.scalar.copy(out=dst, in_=src)
+            else:
+                nc.vector.tensor_copy(out=dst, in_=src)
+
+        def step_h(b, q):
+            words = hn_tiles[b][:].bitcast(F32).rearrange("n (p t q) -> n t q p", t=4, q=8)
+            bank = trp.tile([P, 4, P], F32, name="bank")
+            for t in range(4):
+                nc.tensor.transpose(bank[:, t, :], words[:, t, q, :], ident[:])
+            hb = hbp.tile([P, 2, P, 4], BF16, name="hb", align_bytes=64)
+            hb_tiles[b, q] = hb
+            src = bank[:].rearrange("p t n -> p (t n)").bitcast(BF16).rearrange("p (t n e) -> p e n t", t=4, e=2)
+            nc.vector.tensor_tensor(
+                out=hb[:], in0=src, in1=sc[:].unsqueeze(1).unsqueeze(1).to_broadcast([P, 2, P, 4]), op=ALU.mult
+            )
+
+        def quant_h(b, q):
+            hb = hb_tiles[b, q]
+            for e in range(2):
+                cols = slice(P * b, P * b + P)
+                nc.vector.quantize_mx(
+                    out=hcodes[:, 2 * q + e, cols].bitcast(E4X4),
+                    scales=hscales[:, 2 * q + e, cols],
+                    in_=hb[:, e].rearrange("p n t -> p (n t)"),
+                )
+
+        w_tiles = {}
+
+        def load_w(u):
+            wn = big.tile([P, P, 4, 36], BF16, name="wn", align_bytes=64)
+            for part in range(4):
+                ms = slice(part * 32, (part + 1) * 32)
+                nc.sync.dma_start(out=wn[:, ms].rearrange("p m t k -> p m (t k)"), in_=w_rows[u][:, ms, :])
+            w_tiles[u] = wn
+
+        wb_tiles = {}
+
+        def regroup_w(u, off, engine):
+            wb = wbp.tile([P, 4, P, 4], BF16, name="wb", align_bytes=64)
+            wb_tiles[u, off] = wb
+            src = w_tiles[u][:, :, :, 4 * off : 4 * off + 4]
+            dst = wb[:].rearrange("p k m t -> p m t k")
+            if engine == "S":
+                nc.scalar.copy(out=dst, in_=src)
+            elif engine == "V":
+                nc.vector.tensor_copy(out=dst, in_=src)
+            else:
+                nc.gpsimd.tensor_scalar(out=dst, in0=src, scalar1=1.0, scalar2=0.0, op0=ALU.mult, op1=ALU.add)
+
+        w_codes = {}
+
+        def quant_w(u, off):
+            wc = codes_pool.tile([P, 4, P], U32, name="wc", align_bytes=64)
+            ws = codes_pool.tile([P, 4, P], U8, name="ws", align_bytes=64)
+            nc.vector.quantize_mx(
+                out=wc[:].rearrange("p k m -> p (k m)").bitcast(E4X4),
+                scales=ws[:].rearrange("p k m -> p (k m)"),
+                in_=wb_tiles[u, off][:].rearrange("p k m t -> p (k m t)"),
+            )
+            w_codes[u, off] = (wc, ws)
+
+        accs = {}
+
+        def multiply(u, off, ij, cols, first, last):
+            if (u, ij) not in accs:
+                acc = accp.tile([P, N], F32, name="acc")
+                accs[u, ij] = acc
+            i, j = divmod(ij, 2)
+            di, dj = divmod(off, 3)
+            px = 4 * (i + di) + j + dj
+            wc, ws = w_codes[u, off]
+            nc.tensor.matmul_mx(
+                out=accs[u, ij][:, cols],
+                lhsT=wc[:, ij, :].bitcast(E4X4),
+                lhsT_scale=ws[:, ij, :],
+                rhs=hcodes[:, px, cols].bitcast(E4X4),
+                rhs_scale=hscales[:, px, cols],
+                start=first,
+                stop=last,
+            )
+
+        def multiply_off(u, off, cols):
+            for ij in range(4):
+                multiply(u, off, ij, cols, off == 0, off == OFFS - 1)
+
+        def multiply_by_pixel(u, q, cols):
+            row = q // 2
+            for px in (2 * q, 2 * q + 1):
+                col = px % 4
+                for ij in range(4):
+                    i, j = divmod(ij, 2)
+                    di, dj = row - i, col - j
+                    if 0 <= di <= 2 and 0 <= dj <= 2:
+                        off = 3 * di + dj
+                        multiply(u, off, ij, cols, off == 0, off == OFFS - 1)
+
+        def pool_max(u):
+            best = tail.tile([P, N], F32, name="best")
+            for ij in range(4):
+                bias = b2f[:, 4 * u + ij : 4 * u + ij + 1]
+                if ij == 0:
+                    nc.scalar.activation(out=best[:], in_=accs[u, 0][:], func=ACT.Relu, bias=bias)
+                else:
+                    dst = gbf[:, u, :] if ij == 3 else best[:]
+                    nc.vector.scalar_tensor_tensor(
+                        out=dst, in0=accs[u, ij][:], scalar=bias, in1=best[:], op0=ALU.add, op1=ALU.max
+                    )
+
+        def dense():
+            gis = []
+            for x in range(2):
+                gi = hbp.tile([P, 256, 4], BF16, name="gi", tag="hb", align_bytes=64)
+                nc.vector.tensor_copy(out=gi[:], in_=gbf[:, :, 256 * x : 256 * x + 256].rearrange("p t n -> p n t"))
+                gis.append(gi)
+            for x in range(2):
+                gc = tail.tile([P, 256], U32, name="gc", align_bytes=64)
+                gs = tail.tile([P, 256], U8, name="gs", align_bytes=64)
+                nc.vector.quantize_mx(out=gc[:].bitcast(E4X4), scales=gs[:], in_=gis[x][:].rearrange("p n t -> p (n t)"))
+                for k in range(2):
+                    cols = slice(k * P, (k + 1) * P)
+                    acc_f = accp.tile([P, F], F32, name="acc_f", tag="acc")
+                    nc.tensor.matmul_mx(
+                        out=acc_f[:],
+                        lhsT=gc[:, cols].bitcast(E4X4),
+                        lhsT_scale=gs[:, cols],
+                        rhs=fw[:].bitcast(E2X4),
+                        rhs_scale=fs[:],
+                        start=True,
+                        stop=True,
+                    )
+                    res = tail.tile([P, F], F32, name="res")
+                    nc.vector.tensor_tensor(out=res[:], in0=acc_f[:], in1=fb[:], op=ALU.add)
+                    nc.scalar.activation(out=res[:], in_=res[:], func=ACT.Relu)
+                    row = x * 256 + k * P
+                    nc.sync.dma_start(out=out[row : row + P, :], in_=res[:])
+
+        state = {"unit": 0, "quant": 0, "mm": 0}
+
+        def units(engines):
+            for engine in engines:
+                if state["unit"] < 36:
+                    u, off = divmod(state["unit"], OFFS)
+                    if off == 0 and u >= 1 and u + BIG - 1 < 4:
+                        load_w(u + BIG - 1)
+                    regroup_w(u, off, engine)
+                    state["unit"] += 1
+
+        def quants(lag):
+            while state["quant"] < 36 and state["quant"] + 1 + lag <= state["unit"]:
+                quant_w(*divmod(state["quant"], OFFS))
+                state["quant"] += 1
+
+        x0, x1, full = slice(0, 256), slice(256, 512), slice(0, 512)
+
+        if True:
+            nc.sync.dma_start(out=sc[:], in_=h_scale.rearrange("o (p t) a b -> p (o t a b)", t=4))
+            load_h(0)
+            load_h(1)
+            load_w(0)
+            load_h(2)
+            for u in range(1, BIG):
+                load_w(u)
+            load_h(3)
+            nc.sync.dma_start(out=b2b[:], in_=b2.rearrange("(p t) i j -> p (t i j)", t=4))
+            nc.sync.dma_start(out=fw[:].bitcast(I32), in_=fc1_words.rearrange("g p w -> (g p) w").bitcast(I32))
+            for quad in range(4):
+                nc.sync.dma_start(
+                    out=fs[32 * quad : 32 * quad + 4, :].bitcast(I32),
+                    in_=fc1_scales[0, 4 * quad : 4 * quad + 4, :].bitcast(I32),
+                )
+            nc.sync.dma_start(out=fb[:], in_=fc1_b.partition_broadcast(P))
+            casts = "VSSSSSSS"
+            plan = ["", "", "", "", "", "", "", "S", "", "", "", "", "", "S", "", "S", "", "", "", "", "", "S", "", "S", "S", "", "S", "", "S", "", "S", ""]
+            step = 0
+            for k in range(4):
+                cast_h(k // 2, k % 2, casts[k])
+            last = None
+            for b in range(4):
+                for q in range(8):
+                    step_h(b, q)
+                    if last is not None:
+                        quant_h(*last)
+                    last = (b, q)
+                    units(plan[step])
+                    step += 1
+                    quants(1)
+                    if b >= 2 and q >= 1 and state["mm"] < min(OFFS, state["quant"]):
+                        multiply_off(0, state["mm"], x0)
+                        state["mm"] += 1
+                if b < 2:
+                    for half in range(2):
+                        cast_h(b + 2, half, casts[2 * b + 4 + half])
+                if b == 1:
+                    nc.vector.tensor_copy(out=b2f[:], in_=b2b[:])
+            quant_h(*last)
+            while state["mm"] < OFFS:
+                units("S")
+                quants(0)
+                multiply_off(0, state["mm"], x0)
+                state["mm"] += 1
+            late = ["SV", "V", "SV"]
+            units(late[0])
+            quants(1)
+            for off in range(OFFS):
+                multiply_off(0, off, x1)
+            pool_max(0)
+            step = 1
+            while state["mm"] < 36:
+                units(late[step % len(late)])
+                step += 1
+                quants(1 if state["unit"] < 36 else 0)
+                for dummy in range(1 if state["unit"] < 36 else 36):
+                    if state["mm"] < state["quant"]:
+                        u, off = divmod(state["mm"], OFFS)
+                        multiply_off(u, off, full)
+                        if off == OFFS - 1:
+                            pool_max(u)
+                        state["mm"] += 1
+            dense()

@@ -19,7 +19,9 @@ ACT = mybir.ActivationFunctionType
 
 P = 128
 OFFS = 9
-BIG, HU, HB, WB, WC, TR, AC = 2, 4, 3, 4, 12, 3, 5
+HU, HB, WB, WC, GC = 3, 3, 3, 22, 512
+BY_CHANNEL = (2, 3)
+MM_ORDER = ((0, 0), (1, 0), (0, 1), (1, 1), (2, None), (3, None))
 
 
 def tile_locallyconnectednet_pa_t_w4_kernel(
@@ -27,19 +29,15 @@ def tile_locallyconnectednet_pa_t_w4_kernel(
 ):
     nc = tc.nc
     h_rows = h_bytes.rearrange("(b n) c x y -> b n (c x y)", n=P)
-    w_rows = w2.rearrange("(m u) (p t) k i j -> u p m (t k i j)", u=4, t=4)
+    w_rows = w2.rearrange("(m u) c k i j -> u m (c k i j)", u=4)
+    w_chan = w2.rearrange("(m u) (p t) k i j -> u p m (t k i j)", u=4, t=4)
 
     with ExitStack() as ctx:
         const = ctx.enter_context(tc.tile_pool(name="const", bufs=1))
-        big = ctx.enter_context(tc.tile_pool(name="big", bufs=BIG))
-        hup = ctx.enter_context(tc.tile_pool(name="hup", bufs=HU))
-        hnp = ctx.enter_context(tc.tile_pool(name="hnp", bufs=2))
-        hbp = ctx.enter_context(tc.tile_pool(name="hbp", bufs=HB))
+        big = ctx.enter_context(tc.tile_pool(name="big", bufs=2))
         wbp = ctx.enter_context(tc.tile_pool(name="wbp", bufs=WB))
         codes_pool = ctx.enter_context(tc.tile_pool(name="codes", bufs=WC))
-        tail = ctx.enter_context(tc.tile_pool(name="tail", bufs=2))
-        trp = ctx.enter_context(tc.psum_pool(name="trp", bufs=TR))
-        accp = ctx.enter_context(tc.psum_pool(name="accp", bufs=AC))
+        psum = ctx.enter_context(tc.psum_pool(name="psum", bufs=4))
 
         ident = const.tile([P, P], F32, name="ident")
         make_identity(nc, ident[:])
@@ -54,71 +52,42 @@ def tile_locallyconnectednet_pa_t_w4_kernel(
         fb = const.tile([P, F], BF16, name="fb")
         nc.gpsimd.memset(fs[:].bitcast(I32), 0)
 
-        hu = {}
-        hn_tiles = {}
-        hb_tiles = {}
-
-        def load_h(b):
-            for half in range(2):
-                hu_tile = hup.tile([P, 4096], U8, name="hu", align_bytes=64)
-                nc.sync.dma_start(out=hu_tile[:], in_=h_rows[b][:, half * 4096 : (half + 1) * 4096])
-                hu[b, half] = hu_tile
-
-        def cast_h(b, half, engine):
-            if b not in hn_tiles:
-                hn = hnp.tile([P, 8192], BF16, name="hn", align_bytes=64)
-                hn_tiles[b] = hn
-            src = hu[b, half][:].bitcast(FP8)
-            dst = hn_tiles[b][:, half * 4096 : (half + 1) * 4096]
-            if engine == "S":
-                nc.scalar.copy(out=dst, in_=src)
-            else:
-                nc.vector.tensor_copy(out=dst, in_=src)
-
-        def step_h(b, q):
-            words = hn_tiles[b][:].bitcast(F32).rearrange("n (p t q) -> n t q p", t=4, q=8)
-            bank = trp.tile([P, 4, P], F32, name="bank")
-            for t in range(4):
-                nc.tensor.transpose(bank[:, t, :], words[:, t, q, :], ident[:])
-            hb = hbp.tile([P, 2, P, 4], BF16, name="hb", align_bytes=64)
-            hb_tiles[b, q] = hb
-            src = bank[:].rearrange("p t n -> p (t n)").bitcast(BF16).rearrange("p (t n e) -> p e n t", t=4, e=2)
-            nc.vector.tensor_tensor(
-                out=hb[:], in0=src, in1=sc[:].unsqueeze(1).unsqueeze(1).to_broadcast([P, 2, P, 4]), op=ALU.mult
-            )
-
-        def quant_h(b, q):
-            hb = hb_tiles[b, q]
-            for e in range(2):
-                cols = slice(P * b, P * b + P)
-                nc.vector.quantize_mx(
-                    out=hcodes[:, 2 * q + e, cols].bitcast(E4X4),
-                    scales=hscales[:, 2 * q + e, cols],
-                    in_=hb[:, e].rearrange("p n t -> p (n t)"),
-                )
-
         w_tiles = {}
 
         def load_w(u):
-            wn = big.tile([P, P, 4, 36], BF16, name="wn", align_bytes=64)
+            wn = big.tile([P, C * 36], BF16, name="wn", align_bytes=64)
             for part in range(4):
-                ms = slice(part * 32, (part + 1) * 32)
-                nc.sync.dma_start(out=wn[:, ms].rearrange("p m t k -> p m (t k)"), in_=w_rows[u][:, ms, :])
+                if u in BY_CHANNEL:
+                    ms = slice(part * 32, (part + 1) * 32)
+                    nc.sync.dma_start(out=wn[:].rearrange("p (m x) -> p m x", m=P)[:, ms], in_=w_chan[u][:, ms])
+                else:
+                    cols = slice(part * 4608, (part + 1) * 4608)
+                    nc.sync.dma_start(out=wn[:, cols], in_=w_rows[u][:, cols])
             w_tiles[u] = wn
 
         wb_tiles = {}
 
         def regroup_w(u, off, engine):
-            wb = wbp.tile([P, 4, P, 4], BF16, name="wb", align_bytes=64)
+            wb = wbp.tile([P, 2, 2, P, 4], BF16, name="wb", align_bytes=64)
             wb_tiles[u, off] = wb
-            src = w_tiles[u][:, :, :, 4 * off : 4 * off + 4]
-            dst = wb[:].rearrange("p k m t -> p m t k")
-            if engine == "S":
-                nc.scalar.copy(out=dst, in_=src)
-            elif engine == "V":
-                nc.vector.tensor_copy(out=dst, in_=src)
+            if u in BY_CHANNEL:
+                src = w_tiles[u][:].rearrange("p (m t k) -> p m t k", m=P, t=4)[:, :, :, 4 * off : 4 * off + 4]
+                dst = wb[:].rearrange("p i j m t -> p m t (i j)")
+                if engine == "S":
+                    nc.scalar.copy(out=dst, in_=src)
+                else:
+                    nc.vector.tensor_copy(out=dst, in_=src)
             else:
-                nc.gpsimd.tensor_scalar(out=dst, in0=src, scalar1=1.0, scalar2=0.0, op0=ALU.mult, op1=ALU.add)
+                words = w_tiles[u][:].bitcast(F32).rearrange("m (p t w) -> m t w p", t=4, w=18)
+                for i in range(2):
+                    bank = psum.tile([P, 4, P], F32, name="bank")
+                    for t in range(4):
+                        nc.tensor.transpose(bank[:, t, :], words[:, t, 2 * off + i, :], ident[:])
+                    src = bank[:].rearrange("p t m -> p (t m)").bitcast(BF16).rearrange("p (t m j) -> p j m t", t=4, j=2)
+                    if engine == "S":
+                        nc.scalar.copy(out=wb[:, i], in_=src)
+                    else:
+                        nc.vector.tensor_copy(out=wb[:, i], in_=src)
 
         w_codes = {}
 
@@ -128,84 +97,53 @@ def tile_locallyconnectednet_pa_t_w4_kernel(
             nc.vector.quantize_mx(
                 out=wc[:].rearrange("p k m -> p (k m)").bitcast(E4X4),
                 scales=ws[:].rearrange("p k m -> p (k m)"),
-                in_=wb_tiles[u, off][:].rearrange("p k m t -> p (k m t)"),
+                in_=wb_tiles[u, off][:].rearrange("p i j m t -> p (i j m t)"),
             )
             w_codes[u, off] = (wc, ws)
 
         accs = {}
 
-        def multiply(u, off, ij, cols, first, last):
-            if (u, ij) not in accs:
-                acc = accp.tile([P, N], F32, name="acc")
-                accs[u, ij] = acc
-            i, j = divmod(ij, 2)
+        def acc_of(u, x, ij):
+            if x is None:
+                if (u, ij) not in accs:
+                    acc = psum.tile([P, N], F32, name="acc", tag="acc" if u == 2 else "bank")
+                    accs[u, ij] = acc
+                return accs[u, ij][:]
+            if ("half", x, ij) not in accs:
+                acc = psum.tile([P, 2, 256], F32, name="acc", tag="acc" if x == 0 else "bank")
+                accs["half", x, ij] = acc
+            return accs["half", x, ij][:, u, :]
+
+        def multiply_off(u, off, x):
             di, dj = divmod(off, 3)
-            px = 4 * (i + di) + j + dj
             wc, ws = w_codes[u, off]
-            nc.tensor.matmul_mx(
-                out=accs[u, ij][:, cols],
-                lhsT=wc[:, ij, :].bitcast(E4X4),
-                lhsT_scale=ws[:, ij, :],
-                rhs=hcodes[:, px, cols].bitcast(E4X4),
-                rhs_scale=hscales[:, px, cols],
-                start=first,
-                stop=last,
-            )
-
-        def multiply_off(u, off, cols):
+            cols = slice(0, N) if x is None else slice(256 * x, 256 * x + 256)
             for ij in range(4):
-                multiply(u, off, ij, cols, off == 0, off == OFFS - 1)
+                i, j = divmod(ij, 2)
+                px = 4 * (i + di) + j + dj
+                nc.tensor.matmul_mx(
+                    out=acc_of(u, x, ij),
+                    lhsT=wc[:, ij, :].bitcast(E4X4),
+                    lhsT_scale=ws[:, ij, :],
+                    rhs=hcodes[:, px, cols].bitcast(E4X4),
+                    rhs_scale=hscales[:, px, cols],
+                    start=(off == 0),
+                    stop=(off == OFFS - 1),
+                )
 
-        def multiply_by_pixel(u, q, cols):
-            row = q // 2
-            for px in (2 * q, 2 * q + 1):
-                col = px % 4
-                for ij in range(4):
-                    i, j = divmod(ij, 2)
-                    di, dj = row - i, col - j
-                    if 0 <= di <= 2 and 0 <= dj <= 2:
-                        off = 3 * di + dj
-                        multiply(u, off, ij, cols, off == 0, off == OFFS - 1)
-
-        def pool_max(u):
-            best = tail.tile([P, N], F32, name="best")
+        def pool_max(pool, u, x):
+            cols = slice(0, N) if x is None else slice(256 * x, 256 * x + 256)
+            width = N if x is None else 256
+            best = pool.tile([P, width], F32, name="best")
             for ij in range(4):
                 bias = b2f[:, 4 * u + ij : 4 * u + ij + 1]
                 if ij == 0:
-                    nc.scalar.activation(out=best[:], in_=accs[u, 0][:], func=ACT.Relu, bias=bias)
+                    nc.scalar.activation(out=best[:], in_=acc_of(u, x, 0), func=ACT.Relu, bias=bias)
                 else:
-                    dst = gbf[:, u, :] if ij == 3 else best[:]
+                    dst = gbf[:, u, cols] if ij == 3 else best[:]
                     nc.vector.scalar_tensor_tensor(
-                        out=dst, in0=accs[u, ij][:], scalar=bias, in1=best[:], op0=ALU.add, op1=ALU.max
+                        out=dst, in0=acc_of(u, x, ij), scalar=bias, in1=best[:], op0=ALU.add, op1=ALU.max
                     )
-
-        def dense():
-            gis = []
-            for x in range(2):
-                gi = hbp.tile([P, 256, 4], BF16, name="gi", tag="hb", align_bytes=64)
-                nc.vector.tensor_copy(out=gi[:], in_=gbf[:, :, 256 * x : 256 * x + 256].rearrange("p t n -> p n t"))
-                gis.append(gi)
-            for x in range(2):
-                gc = tail.tile([P, 256], U32, name="gc", align_bytes=64)
-                gs = tail.tile([P, 256], U8, name="gs", align_bytes=64)
-                nc.vector.quantize_mx(out=gc[:].bitcast(E4X4), scales=gs[:], in_=gis[x][:].rearrange("p n t -> p (n t)"))
-                for k in range(2):
-                    cols = slice(k * P, (k + 1) * P)
-                    acc_f = accp.tile([P, F], F32, name="acc_f", tag="acc")
-                    nc.tensor.matmul_mx(
-                        out=acc_f[:],
-                        lhsT=gc[:, cols].bitcast(E4X4),
-                        lhsT_scale=gs[:, cols],
-                        rhs=fw[:].bitcast(E2X4),
-                        rhs_scale=fs[:],
-                        start=True,
-                        stop=True,
-                    )
-                    res = tail.tile([P, F], F32, name="res")
-                    nc.vector.tensor_tensor(out=res[:], in0=acc_f[:], in1=fb[:], op=ALU.add)
-                    nc.scalar.activation(out=res[:], in_=res[:], func=ACT.Relu)
-                    row = x * 256 + k * P
-                    nc.sync.dma_start(out=out[row : row + P, :], in_=res[:])
 
         state = {"unit": 0, "quant": 0, "mm": 0}
 
@@ -213,80 +151,160 @@ def tile_locallyconnectednet_pa_t_w4_kernel(
             for engine in engines:
                 if state["unit"] < 36:
                     u, off = divmod(state["unit"], OFFS)
-                    if off == 0 and u >= 1 and u + BIG - 1 < 4:
-                        load_w(u + BIG - 1)
                     regroup_w(u, off, engine)
                     state["unit"] += 1
+                    if off == OFFS - 1 and u < 2:
+                        load_w(u + 2)
 
         def quants(lag):
             while state["quant"] < 36 and state["quant"] + 1 + lag <= state["unit"]:
                 quant_w(*divmod(state["quant"], OFFS))
                 state["quant"] += 1
 
-        x0, x1, full = slice(0, 256), slice(256, 512), slice(0, 512)
+        todo = [(u, off, x) for u, x in MM_ORDER for off in range(OFFS)]
 
-        if True:
-            nc.sync.dma_start(out=sc[:], in_=h_scale.rearrange("o (p t) a b -> p (o t a b)", t=4))
-            load_h(0)
-            load_h(1)
-            load_w(0)
-            load_h(2)
-            for u in range(1, BIG):
-                load_w(u)
-            load_h(3)
-            nc.sync.dma_start(out=b2b[:], in_=b2.rearrange("(p t) i j -> p (t i j)", t=4))
-            nc.sync.dma_start(out=fw[:].bitcast(I32), in_=fc1_words.rearrange("g p w -> (g p) w").bitcast(I32))
-            for quad in range(4):
-                nc.sync.dma_start(
-                    out=fs[32 * quad : 32 * quad + 4, :].bitcast(I32),
-                    in_=fc1_scales[0, 4 * quad : 4 * quad + 4, :].bitcast(I32),
-                )
-            nc.sync.dma_start(out=fb[:], in_=fc1_b.partition_broadcast(P))
-            casts = "VSSSSSSS"
-            plan = ["", "", "", "", "", "", "", "S", "", "", "", "", "", "S", "", "S", "", "", "", "", "", "S", "", "S", "S", "", "S", "", "S", "", "S", ""]
-            step = 0
-            for k in range(4):
-                cast_h(k // 2, k % 2, casts[k])
-            last = None
-            for b in range(4):
-                for q in range(8):
-                    step_h(b, q)
-                    if last is not None:
-                        quant_h(*last)
-                    last = (b, q)
-                    units(plan[step])
-                    step += 1
-                    quants(1)
-                    if b >= 2 and q >= 1 and state["mm"] < min(OFFS, state["quant"]):
-                        multiply_off(0, state["mm"], x0)
-                        state["mm"] += 1
-                if b < 2:
+        def matmuls(count, h_half, lag):
+            for dummy in range(count):
+                if state["mm"] < len(todo):
+                    u, off, x = todo[state["mm"]]
+                    if (x is None or x == 1) and h_half < 2:
+                        return
+                    if OFFS * u + off + 1 + lag > state["quant"]:
+                        return
+                    multiply_off(u, off, x)
+                    state["mm"] += 1
+                    if off == OFFS - 1:
+                        finished.append((u, x))
+
+        finished = []
+
+        with ExitStack():
+            with ExitStack() as early:
+                hup = early.enter_context(tc.tile_pool(name="hup", bufs=HU))
+                hnp = early.enter_context(tc.tile_pool(name="hnp", bufs=2))
+                hbp = early.enter_context(tc.tile_pool(name="hbp", bufs=HB))
+                hu = {}
+                hn_tiles = {}
+                hb_tiles = {}
+
+                def load_h(b):
                     for half in range(2):
-                        cast_h(b + 2, half, casts[2 * b + 4 + half])
-                if b == 1:
-                    nc.vector.tensor_copy(out=b2f[:], in_=b2b[:])
-            quant_h(*last)
-            while state["mm"] < OFFS:
-                units("S")
-                quants(0)
-                multiply_off(0, state["mm"], x0)
-                state["mm"] += 1
-            late = ["SV", "V", "SV"]
-            units(late[0])
-            quants(1)
-            for off in range(OFFS):
-                multiply_off(0, off, x1)
-            pool_max(0)
-            step = 1
-            while state["mm"] < 36:
-                units(late[step % len(late)])
-                step += 1
-                quants(1 if state["unit"] < 36 else 0)
-                for dummy in range(1 if state["unit"] < 36 else 36):
-                    if state["mm"] < state["quant"]:
-                        u, off = divmod(state["mm"], OFFS)
-                        multiply_off(u, off, full)
-                        if off == OFFS - 1:
-                            pool_max(u)
-                        state["mm"] += 1
-            dense()
+                        hu_tile = hup.tile([P, 4096], U8, name="hu", align_bytes=64)
+                        nc.sync.dma_start(out=hu_tile[:], in_=h_rows[b][:, half * 4096 : (half + 1) * 4096])
+                        hu[b, half] = hu_tile
+
+                def cast_h(b, half, engine):
+                    if b not in hn_tiles:
+                        hn = hnp.tile([P, 8192], BF16, name="hn", align_bytes=64)
+                        hn_tiles[b] = hn
+                    src = hu[b, half][:].bitcast(FP8)
+                    dst = hn_tiles[b][:, half * 4096 : (half + 1) * 4096]
+                    if engine == "S":
+                        nc.scalar.copy(out=dst, in_=src)
+                    elif engine == "V":
+                        nc.vector.tensor_copy(out=dst, in_=src)
+                    else:
+                        for k in range(0, 4096, GC):
+                            nc.gpsimd.tensor_copy(out=dst[:, k : k + GC], in_=src[:, k : k + GC])
+
+                def step_h(b, q):
+                    words = hn_tiles[b][:].bitcast(F32).rearrange("n (p t q) -> n t q p", t=4, q=8)
+                    bank = psum.tile([P, 4, P], F32, name="bank")
+                    for t in range(4):
+                        nc.tensor.transpose(bank[:, t, :], words[:, t, q, :], ident[:])
+                    hb = hbp.tile([P, 2, P, 4], BF16, name="hb", align_bytes=64)
+                    hb_tiles[b, q] = hb
+                    src = bank[:].rearrange("p t n -> p (t n)").bitcast(BF16).rearrange("p (t n e) -> p e n t", t=4, e=2)
+                    nc.vector.tensor_tensor(
+                        out=hb[:], in0=src, in1=sc[:].unsqueeze(1).unsqueeze(1).to_broadcast([P, 2, P, 4]), op=ALU.mult
+                    )
+
+                def quant_h(b, q):
+                    hb = hb_tiles[b, q]
+                    for e in range(2):
+                        cols = slice(P * b, P * b + P)
+                        nc.vector.quantize_mx(
+                            out=hcodes[:, 2 * q + e, cols].bitcast(E4X4),
+                            scales=hscales[:, 2 * q + e, cols],
+                            in_=hb[:, e].rearrange("p n t -> p (n t)"),
+                        )
+
+                nc.sync.dma_start(out=sc[:], in_=h_scale.rearrange("o (p t) a b -> p (o t a b)", t=4))
+                load_h(0)
+                load_h(1)
+                load_h(2)
+                load_w(0)
+                load_h(3)
+                nc.sync.dma_start(out=b2b[:], in_=b2.rearrange("(p t) i j -> p (t i j)", t=4))
+                load_w(1)
+                nc.sync.dma_start(out=fw[:].bitcast(I32), in_=fc1_words.rearrange("g p w -> (g p) w").bitcast(I32))
+                for quad in range(4):
+                    nc.sync.dma_start(
+                        out=fs[32 * quad : 32 * quad + 4, :].bitcast(I32),
+                        in_=fc1_scales[0, 4 * quad : 4 * quad + 4, :].bitcast(I32),
+                    )
+                nc.sync.dma_start(out=fb[:], in_=fc1_b.partition_broadcast(P))
+                casts = "VVSSGGGG"
+                plan = ["","","","","","","S","S","","S","S","","S","S","","S","S","","S","S","","S","S","","S","S","","S","S","","S","S"]
+                for k in range(4):
+                    cast_h(k // 2, k % 2, casts[k])
+                order = [(b, q) for b in range(4) for q in range(8)]
+                for step in range(32):
+                    b, q = order[step]
+                    step_h(b, q)
+                    if step >= 1:
+                        quant_h(*order[step - 1])
+                    units(plan[step])
+                    quants(1)
+                    if q == 7 and b < 2:
+                        for half in range(2):
+                            cast_h(b + 2, half, casts[2 * b + 4 + half])
+                    if step == 20:
+                        nc.vector.tensor_copy(out=b2f[:], in_=b2b[:])
+                    if step >= 18:
+                        matmuls(1, 1, 2)
+                quant_h(*order[31])
+            with ExitStack() as last:
+                tail = last.enter_context(tc.tile_pool(name="tail", bufs=2))
+                late = ["S", "V"]
+                step = 0
+                pend = []
+                while state["mm"] < len(todo):
+                    units(late[step % len(late)])
+                    step += 1
+                    quants(1 if state["unit"] < 36 else 0)
+                    for u, x in finished:
+                        pool_max(tail, u, x)
+                    while len(finished) > 0:
+                        finished.remove(finished[0])
+                    matmuls(2 if state["unit"] < 36 else 36, 2, 0)
+                for u, x in finished:
+                    pool_max(tail, u, x)
+                gis = []
+                for x in range(2):
+                    gi = tail.tile([P, 256, 4], BF16, name="gi", align_bytes=64)
+                    nc.vector.tensor_copy(out=gi[:], in_=gbf[:, :, 256 * x : 256 * x + 256].rearrange("p t n -> p n t"))
+                    gis.append(gi)
+                for x in range(2):
+                    gc = tail.tile([P, 256], U32, name="gc", align_bytes=64)
+                    gs = tail.tile([P, 256], U8, name="gs", align_bytes=64)
+                    nc.vector.quantize_mx(
+                        out=gc[:].bitcast(E4X4), scales=gs[:], in_=gis[x][:].rearrange("p n t -> p (n t)")
+                    )
+                    for k in range(2):
+                        cols = slice(k * P, (k + 1) * P)
+                        acc_f = psum.tile([P, F], F32, name="acc_f", tag="acc")
+                        nc.tensor.matmul_mx(
+                            out=acc_f[:],
+                            lhsT=gc[:, cols].bitcast(E4X4),
+                            lhsT_scale=gs[:, cols],
+                            rhs=fw[:].bitcast(E2X4),
+                            rhs_scale=fs[:],
+                            start=True,
+                            stop=True,
+                        )
+                        res = tail.tile([P, F], F32, name="res", bufs=4)
+                        nc.vector.tensor_tensor(out=res[:], in0=acc_f[:], in1=fb[:], op=ALU.add)
+                        nc.scalar.activation(out=res[:], in_=res[:], func=ACT.Relu)
+                        row = x * 256 + k * P
+                        nc.sync.dma_start(out=out[row : row + P, :], in_=res[:])

from contextlib import ExitStack

import concourse.mybir as mybir
from concourse.masks import make_identity

N, C, PX, O, F = 512, 512, 16, 512, 512
FLOPS = 2 * N * C * 9 * 4 * O + 2 * N * O * F

F32 = mybir.dt.float32
BF16 = mybir.dt.bfloat16
U32 = mybir.dt.uint32
I32 = mybir.dt.int32
U8 = mybir.dt.uint8
FP8 = mybir.dt.float8_e4m3fn
E4X4 = mybir.dt.float8_e4m3fn_x4
E2X4 = mybir.dt.float4_e2m1fn_x4
ALU = mybir.AluOpType
ACT = mybir.ActivationFunctionType

P = 128
OFFS = 9
HU, HB, WB, WC, GC = 3, 3, 3, 22, 512
BY_CHANNEL = (2, 3)
MM_ORDER = ((0, 0), (1, 0), (0, 1), (1, 1), (2, None), (3, None))


def tile_locallyconnectednet_pa_t_w4_kernel(
    tc, h_bytes, h_scale, w2, b2, fc1_words, fc1_scales, fc1_b, out
):
    nc = tc.nc
    h_rows = h_bytes.rearrange("(b n) c x y -> b n (c x y)", n=P)
    w_rows = w2.rearrange("(m u) c k i j -> u m (c k i j)", u=4)
    w_chan = w2.rearrange("(m u) (p t) k i j -> u p m (t k i j)", u=4, t=4)

    with ExitStack() as ctx:
        const = ctx.enter_context(tc.tile_pool(name="const", bufs=1))
        big = ctx.enter_context(tc.tile_pool(name="big", bufs=2))
        wbp = ctx.enter_context(tc.tile_pool(name="wbp", bufs=WB))
        codes_pool = ctx.enter_context(tc.tile_pool(name="codes", bufs=WC))
        psum = ctx.enter_context(tc.psum_pool(name="psum", bufs=4))

        ident = const.tile([P, P], F32, name="ident")
        make_identity(nc, ident[:])
        sc = const.tile([P, 4], F32, name="sc")
        hcodes = const.tile([P, PX, N], U32, name="hcodes", align_bytes=64)
        hscales = const.tile([P, PX, N], U8, name="hscales", align_bytes=64)
        gbf = const.tile([P, 4, N], BF16, name="gbf", align_bytes=64)
        b2b = const.tile([P, 16], BF16, name="b2b")
        b2f = const.tile([P, 16], F32, name="b2f")
        fw = const.tile([P, 1024], U8, name="fw", align_bytes=64)
        fs = const.tile([P, F], U8, name="fs", align_bytes=64)
        fb = const.tile([P, F], BF16, name="fb")
        nc.gpsimd.memset(fs[:].bitcast(I32), 0)

        w_tiles = {}

        def load_w(u):
            wn = big.tile([P, C * 36], BF16, name="wn", align_bytes=64)
            for part in range(4):
                if u in BY_CHANNEL:
                    ms = slice(part * 32, (part + 1) * 32)
                    nc.sync.dma_start(out=wn[:].rearrange("p (m x) -> p m x", m=P)[:, ms], in_=w_chan[u][:, ms])
                else:
                    cols = slice(part * 4608, (part + 1) * 4608)
                    nc.sync.dma_start(out=wn[:, cols], in_=w_rows[u][:, cols])
            w_tiles[u] = wn

        wb_tiles = {}

        def regroup_w(u, off, engine):
            wb = wbp.tile([P, 2, 2, P, 4], BF16, name="wb", align_bytes=64)
            wb_tiles[u, off] = wb
            if u in BY_CHANNEL:
                src = w_tiles[u][:].rearrange("p (m t k) -> p m t k", m=P, t=4)[:, :, :, 4 * off : 4 * off + 4]
                dst = wb[:].rearrange("p i j m t -> p m t (i j)")
                if engine == "S":
                    nc.scalar.copy(out=dst, in_=src)
                else:
                    nc.vector.tensor_copy(out=dst, in_=src)
            else:
                words = w_tiles[u][:].bitcast(F32).rearrange("m (p t w) -> m t w p", t=4, w=18)
                for i in range(2):
                    bank = psum.tile([P, 4, P], F32, name="bank")
                    for t in range(4):
                        nc.tensor.transpose(bank[:, t, :], words[:, t, 2 * off + i, :], ident[:])
                    src = bank[:].rearrange("p t m -> p (t m)").bitcast(BF16).rearrange("p (t m j) -> p j m t", t=4, j=2)
                    if engine == "S":
                        nc.scalar.copy(out=wb[:, i], in_=src)
                    else:
                        nc.vector.tensor_copy(out=wb[:, i], in_=src)

        w_codes = {}

        def quant_w(u, off):
            wc = codes_pool.tile([P, 4, P], U32, name="wc", align_bytes=64)
            ws = codes_pool.tile([P, 4, P], U8, name="ws", align_bytes=64)
            nc.vector.quantize_mx(
                out=wc[:].rearrange("p k m -> p (k m)").bitcast(E4X4),
                scales=ws[:].rearrange("p k m -> p (k m)"),
                in_=wb_tiles[u, off][:].rearrange("p i j m t -> p (i j m t)"),
            )
            w_codes[u, off] = (wc, ws)

        accs = {}

        def acc_of(u, x, ij):
            if x is None:
                if (u, ij) not in accs:
                    acc = psum.tile([P, N], F32, name="acc", tag="acc" if u == 2 else "bank")
                    accs[u, ij] = acc
                return accs[u, ij][:]
            if ("half", x, ij) not in accs:
                acc = psum.tile([P, 2, 256], F32, name="acc", tag="acc" if x == 0 else "bank")
                accs["half", x, ij] = acc
            return accs["half", x, ij][:, u, :]

        def multiply_off(u, off, x):
            di, dj = divmod(off, 3)
            wc, ws = w_codes[u, off]
            cols = slice(0, N) if x is None else slice(256 * x, 256 * x + 256)
            for ij in range(4):
                i, j = divmod(ij, 2)
                px = 4 * (i + di) + j + dj
                nc.tensor.matmul_mx(
                    out=acc_of(u, x, ij),
                    lhsT=wc[:, ij, :].bitcast(E4X4),
                    lhsT_scale=ws[:, ij, :],
                    rhs=hcodes[:, px, cols].bitcast(E4X4),
                    rhs_scale=hscales[:, px, cols],
                    start=(off == 0),
                    stop=(off == OFFS - 1),
                )

        def pool_max(pool, u, x):
            cols = slice(0, N) if x is None else slice(256 * x, 256 * x + 256)
            width = N if x is None else 256
            best = pool.tile([P, width], F32, name="best")
            for ij in range(4):
                bias = b2f[:, 4 * u + ij : 4 * u + ij + 1]
                if ij == 0:
                    nc.scalar.activation(out=best[:], in_=acc_of(u, x, 0), func=ACT.Relu, bias=bias)
                else:
                    dst = gbf[:, u, cols] if ij == 3 else best[:]
                    nc.vector.scalar_tensor_tensor(
                        out=dst, in0=acc_of(u, x, ij), scalar=bias, in1=best[:], op0=ALU.add, op1=ALU.max
                    )

        state = {"unit": 0, "quant": 0, "mm": 0}

        def units(engines):
            for engine in engines:
                if state["unit"] < 36:
                    u, off = divmod(state["unit"], OFFS)
                    regroup_w(u, off, engine)
                    state["unit"] += 1
                    if off == OFFS - 1 and u < 2:
                        load_w(u + 2)

        def quants(lag):
            while state["quant"] < 36 and state["quant"] + 1 + lag <= state["unit"]:
                quant_w(*divmod(state["quant"], OFFS))
                state["quant"] += 1

        todo = [(u, off, x) for u, x in MM_ORDER for off in range(OFFS)]

        def matmuls(count, h_half, lag):
            for dummy in range(count):
                if state["mm"] < len(todo):
                    u, off, x = todo[state["mm"]]
                    if (x is None or x == 1) and h_half < 2:
                        return
                    if OFFS * u + off + 1 + lag > state["quant"]:
                        return
                    multiply_off(u, off, x)
                    state["mm"] += 1
                    if off == OFFS - 1:
                        finished.append((u, x))

        finished = []

        with ExitStack():
            with ExitStack() as early:
                hup = early.enter_context(tc.tile_pool(name="hup", bufs=HU))
                hnp = early.enter_context(tc.tile_pool(name="hnp", bufs=2))
                hbp = early.enter_context(tc.tile_pool(name="hbp", bufs=HB))
                hu = {}
                hn_tiles = {}
                hb_tiles = {}

                def load_h(b):
                    for half in range(2):
                        hu_tile = hup.tile([P, 4096], U8, name="hu", align_bytes=64)
                        nc.sync.dma_start(out=hu_tile[:], in_=h_rows[b][:, half * 4096 : (half + 1) * 4096])
                        hu[b, half] = hu_tile

                def cast_h(b, half, engine):
                    if b not in hn_tiles:
                        hn = hnp.tile([P, 8192], BF16, name="hn", align_bytes=64)
                        hn_tiles[b] = hn
                    src = hu[b, half][:].bitcast(FP8)
                    dst = hn_tiles[b][:, half * 4096 : (half + 1) * 4096]
                    if engine == "S":
                        nc.scalar.copy(out=dst, in_=src)
                    elif engine == "V":
                        nc.vector.tensor_copy(out=dst, in_=src)
                    else:
                        for k in range(0, 4096, GC):
                            nc.gpsimd.tensor_copy(out=dst[:, k : k + GC], in_=src[:, k : k + GC])

                def step_h(b, q):
                    words = hn_tiles[b][:].bitcast(F32).rearrange("n (p t q) -> n t q p", t=4, q=8)
                    bank = psum.tile([P, 4, P], F32, name="bank")
                    for t in range(4):
                        nc.tensor.transpose(bank[:, t, :], words[:, t, q, :], ident[:])
                    hb = hbp.tile([P, 2, P, 4], BF16, name="hb", align_bytes=64)
                    hb_tiles[b, q] = hb
                    src = bank[:].rearrange("p t n -> p (t n)").bitcast(BF16).rearrange("p (t n e) -> p e n t", t=4, e=2)
                    nc.vector.tensor_tensor(
                        out=hb[:], in0=src, in1=sc[:].unsqueeze(1).unsqueeze(1).to_broadcast([P, 2, P, 4]), op=ALU.mult
                    )

                def quant_h(b, q):
                    hb = hb_tiles[b, q]
                    for e in range(2):
                        cols = slice(P * b, P * b + P)
                        nc.vector.quantize_mx(
                            out=hcodes[:, 2 * q + e, cols].bitcast(E4X4),
                            scales=hscales[:, 2 * q + e, cols],
                            in_=hb[:, e].rearrange("p n t -> p (n t)"),
                        )

                nc.sync.dma_start(out=sc[:], in_=h_scale.rearrange("o (p t) a b -> p (o t a b)", t=4))
                load_h(0)
                load_h(1)
                load_h(2)
                load_w(0)
                load_h(3)
                nc.sync.dma_start(out=b2b[:], in_=b2.rearrange("(p t) i j -> p (t i j)", t=4))
                load_w(1)
                nc.sync.dma_start(out=fw[:].bitcast(I32), in_=fc1_words.rearrange("g p w -> (g p) w").bitcast(I32))
                for quad in range(4):
                    nc.sync.dma_start(
                        out=fs[32 * quad : 32 * quad + 4, :].bitcast(I32),
                        in_=fc1_scales[0, 4 * quad : 4 * quad + 4, :].bitcast(I32),
                    )
                nc.sync.dma_start(out=fb[:], in_=fc1_b.partition_broadcast(P))
                casts = "VVSSGGGG"
                plan = ["","","","","","","S","S","","S","S","","S","S","","S","S","","S","S","","S","S","","S","S","","S","S","","S","S"]
                for k in range(4):
                    cast_h(k // 2, k % 2, casts[k])
                order = [(b, q) for b in range(4) for q in range(8)]
                for step in range(32):
                    b, q = order[step]
                    step_h(b, q)
                    if step >= 1:
                        quant_h(*order[step - 1])
                    units(plan[step])
                    quants(1)
                    if q == 7 and b < 2:
                        for half in range(2):
                            cast_h(b + 2, half, casts[2 * b + 4 + half])
                    if step == 20:
                        nc.vector.tensor_copy(out=b2f[:], in_=b2b[:])
                    if step >= 18:
                        matmuls(1, 1, 2)
                quant_h(*order[31])
            with ExitStack() as last:
                tail = last.enter_context(tc.tile_pool(name="tail", bufs=2))
                late = ["S", "V"]
                step = 0
                pend = []
                while state["mm"] < len(todo):
                    units(late[step % len(late)])
                    step += 1
                    quants(1 if state["unit"] < 36 else 0)
                    for u, x in finished:
                        pool_max(tail, u, x)
                    while len(finished) > 0:
                        finished.remove(finished[0])
                    matmuls(2 if state["unit"] < 36 else 36, 2, 0)
                for u, x in finished:
                    pool_max(tail, u, x)
                gis = []
                for x in range(2):
                    gi = tail.tile([P, 256, 4], BF16, name="gi", align_bytes=64)
                    nc.vector.tensor_copy(out=gi[:], in_=gbf[:, :, 256 * x : 256 * x + 256].rearrange("p t n -> p n t"))
                    gis.append(gi)
                for x in range(2):
                    gc = tail.tile([P, 256], U32, name="gc", align_bytes=64)
                    gs = tail.tile([P, 256], U8, name="gs", align_bytes=64)
                    nc.vector.quantize_mx(
                        out=gc[:].bitcast(E4X4), scales=gs[:], in_=gis[x][:].rearrange("p n t -> p (n t)")
                    )
                    for k in range(2):
                        cols = slice(k * P, (k + 1) * P)
                        acc_f = psum.tile([P, F], F32, name="acc_f", tag="acc")
                        nc.tensor.matmul_mx(
                            out=acc_f[:],
                            lhsT=gc[:, cols].bitcast(E4X4),
                            lhsT_scale=gs[:, cols],
                            rhs=fw[:].bitcast(E2X4),
                            rhs_scale=fs[:],
                            start=True,
                            stop=True,
                        )
                        res = tail.tile([P, F], F32, name="res", bufs=4)
                        nc.vector.tensor_tensor(out=res[:], in0=acc_f[:], in1=fb[:], op=ALU.add)
                        nc.scalar.activation(out=res[:], in_=res[:], func=ACT.Relu)
                        row = x * 256 + k * P
                        nc.sync.dma_start(out=out[row : row + P, :], in_=res[:])
